import numpy as np
import ml_dtypes


def mxq(x, axis, fmt="e4m3"):
    dtype, down = {"e4m3": (ml_dtypes.float8_e4m3fn, 7), "e5m2": (ml_dtypes.float8_e5m2, 14)}[fmt]
    v = np.moveaxis(np.asarray(x, np.float32).astype(ml_dtypes.bfloat16).astype(np.float64), axis, -1)
    blocks = v.reshape(v.shape[:-1] + (-1, 32))
    amax = np.abs(blocks).max(-1, keepdims=True)
    byte = np.maximum(np.where(amax > 0, np.frexp(amax)[1] - 1 + 127, 0) - down, 1)
    scale = np.exp2(byte - 127.0)
    codes = (blocks / scale).astype(np.float32).astype(dtype).astype(np.float64)
    return np.moveaxis((codes * scale).reshape(v.shape), -1, axis)


WIDE = False


def mx_kscale(k):
    if not WIDE:
        return np.ones(k)
    levels = np.array([10, -10, 5, -5, 0])
    if k % 512:
        return np.exp2(np.random.permutation(np.resize(levels, k // 32))).repeat(32)
    a = np.empty((k // 512, 16))
    for p in range(k // 512):
        a[p, :8] = np.random.permutation(np.resize(levels, 8))
        for g in range(8):
            far = levels[np.abs(levels - a[p, g]) >= 10]
            a[p, g + 8] = far[np.random.randint(len(far))]
    return np.exp2(a.ravel()).repeat(32)


BF16 = ml_dtypes.bfloat16


def bf(x):
    return np.asarray(x, np.float32).astype(BF16)


def f64(x):
    return np.asarray(x).astype(np.float64)


BQ, BK, L, H, DH = 4, 4, 512, 4, 128
D = H * DH


def setup_inputs():
    s, t = mx_kscale(D), mx_kscale(D)
    amp_q = 0.5 + np.random.random((BQ, 1, 1))
    amp_k = 0.5 + np.random.random((BK, 1, 1))
    return {
        "query_states": bf(np.random.standard_normal((BQ, L, D)) * amp_q * s),
        "key_states": bf(np.random.standard_normal((BK, L, D)) * amp_k * s),
        "Wq": bf(np.random.standard_normal((D, D)) * 0.8 / np.sqrt(D) * t[:, None] / s[None, :]),
        "bq": bf(np.random.standard_normal(D) * 0.3 * t),
        "Wk": bf(np.random.standard_normal((D, D)) * 0.8 / np.sqrt(D) / t[:, None] / s[None, :]),
        "bk": bf(np.random.standard_normal(D) * 0.3 / t),
        "logit_scale": bf(-1.5 + 0.1 * np.random.standard_normal(1)),
    }


def reference(query_states, key_states, Wq, bq, Wk, bk, logit_scale):
    q = f64(bf(mxq(f64(query_states).reshape(BQ * L, D), 1, "e4m3") @ mxq(f64(Wq), 1, "e4m3").T)) + f64(bq)
    k = f64(bf(mxq(f64(key_states).reshape(BK * L, D), 1, "e4m3") @ mxq(f64(Wk), 1, "e4m3").T)) + f64(bk)
    retrieve = mxq(q, 1, "e4m3") @ mxq(k, 1, "e4m3").T
    retrieve = retrieve.reshape(BQ, L, BK, L).transpose(0, 2, 1, 3)
    t2v = retrieve.max(axis=-1).sum(axis=2) / L
    v2t = retrieve.max(axis=-2).sum(axis=2) / L
    return np.exp(f64(logit_scale)) * (t2v + v2t) / 2.0

@@ -1,0 +1,264 @@
+from contextlib import ExitStack
+
+import concourse.mybir as mybir
+from concourse.masks import make_identity
+
+F32 = mybir.dt.float32
+BF16 = mybir.dt.bfloat16
+U32 = mybir.dt.uint32
+U8 = mybir.dt.uint8
+FP8X4 = mybir.dt.float8_e4m3fn_x4
+ALU = mybir.AluOpType
+ACT = mybir.ActivationFunctionType
+AX = mybir.AxisListType
+
+P = 128
+NS = 4
+L = 512
+D = 512
+NT = L // P
+BANK_DT = BF16
+LOOKAHEAD = 4
+
+FLOPS = 2 * (2 * NS * L) * D * D + 2 * (NS * L) * (NS * L) * D
+
+
+def tile_attention_pa_kernel(tc, query_states, key_states, Wq, bq, Wk, bk, logit_scale, out):
+    nc = tc.nc
+    with ExitStack() as ctx:
+        const = ctx.enter_context(tc.tile_pool(name="const", bufs=1))
+        xin_pool = ctx.enter_context(tc.tile_pool(name="xin", bufs=1))
+        keep = ctx.enter_context(tc.tile_pool(name="keep", bufs=1))
+        work = ctx.enter_context(tc.tile_pool(name="work", bufs=3))
+        psum_f = ctx.enter_context(tc.psum_pool(name="psum_f", bufs=3))
+        psum_r = ctx.enter_context(tc.psum_pool(name="psum_r", bufs=5))
+
+        units = [
+            (Wk, True, 0, 0),
+            (key_states[0], False, 0, 4),
+            (Wq, True, 2, 0),
+            (query_states[0], False, 2, 0),
+        ]
+        for s in range(1, NS):
+            units.append((key_states[s], False, 0, 4))
+            units.append((query_states[s], False, 2, 0))
+
+        ls_raw = const.tile([P, 1], BF16, name="ls_raw", tag="ls_raw")
+        nc.scalar.dma_start(out=ls_raw[:], in_=logit_scale.partition_broadcast(P))
+        bq_raw = const.tile([P, 4], BF16, name="bq_raw", tag="bq_raw")
+        nc.scalar.dma_start(out=bq_raw[:], in_=bq.rearrange("(p t) -> p t", t=4))
+        bk_raw = const.tile([P, 4], BF16, name="bk_raw", tag="bk_raw")
+        nc.scalar.dma_start(out=bk_raw[:], in_=bk.rearrange("(p t) -> p t", t=4))
+
+        xin = []
+        for u in range(len(units)):
+            x_sb = xin_pool.tile([P, NT, D], BF16, name="xin%d" % u, tag="xin%d" % u)
+            rows = units[u][0].rearrange("(p n) k -> p n k", n=NT)
+            for h in range(2):
+                nc.sync.dma_start(out=x_sb[:, 2 * h:2 * h + 2, :], in_=rows[:, 2 * h:2 * h + 2, :])
+            xin.append(x_sb)
+
+        ident = const.tile([P, P], F32, name="ident", tag="ident")
+        make_identity(nc, ident[:])
+        gain = const.tile([P, 1], F32, name="gain", tag="gain")
+        nc.scalar.activation(out=gain[:], in_=ls_raw[:], func=ACT.Exp)
+        bias = const.tile([P, 8], F32, name="bias", tag="bias")
+        nc.vector.tensor_copy(out=bias[:, 0:4], in_=bq_raw[:])
+        nc.vector.tensor_copy(out=bias[:, 4:8], in_=bk_raw[:])
+        sel = const.tile([P, 2, P], F32, name="sel", tag="sel")
+        nc.vector.memset(sel[:], 0.0)
+        nc.vector.memset(sel[:, 0, 0:1], 1.0)
+        nc.vector.memset(sel[:, 1, 1:2], 1.0)
+        stats = const.tile([P, NS * NS, 8], F32, name="stats", tag="stats")
+
+        grouped = {}
+        xbank = {}
+        codes = {}
+        scales = {}
+        xcodes = {}
+        xscales = {}
+        pbank = {}
+        ycont = {}
+        yint = {}
+        rbank = {}
+
+        def transposes(u, h):
+            words = xin[u][:].bitcast(F32)
+            xt = psum_f.tile([P, 512], F32, name="xt", tag="front")
+            for n in range(2):
+                for w in range(2):
+                    c0 = (2 * n + w) * P
+                    nc.tensor.transpose(xt[:, c0:c0 + P], words[:, 2 * h + n, w:D // 2:2], ident[:])
+            xbank[(u, h)] = xt
+
+        def group(u, h, eng):
+            if h == 0:
+                grouped[u] = work.tile([P, 4 * L], BF16, name="grouped", tag="grouped", align_bytes=64)
+            dst = grouped[u][:].bitcast(F32)[:, 512 * h:512 * (h + 1)].rearrange("p (n r w) -> p n r w", n=2, w=2)
+            src = xbank[(u, h)][:].rearrange("p (n w r) -> p n r w", n=2, w=2)
+            if eng == "V":
+                nc.vector.tensor_copy(out=dst, in_=src)
+            else:
+                nc.scalar.copy(out=dst, in_=src)
+
+        def quantize_in(u):
+            if units[u][1]:
+                xc = keep.tile([P, L], U32, name="wc%d" % u, tag="wc%d" % u, align_bytes=64)
+                xs = keep.tile([P, L], U8, name="ws%d" % u, tag="ws%d" % u, align_bytes=64)
+            else:
+                xc = work.tile([P, L], U32, name="xc", tag="xc", align_bytes=64)
+                xs = work.tile([P, L], U8, name="xs", tag="xs", align_bytes=64)
+            nc.vector.quantize_mx(out=xc[:].bitcast(FP8X4), scales=xs[:], in_=grouped[u][:])
+            xcodes[u] = xc
+            xscales[u] = xs
+
+        def project(u, t):
+            w_unit = units[u][2]
+            pb = psum_f.tile([P, L], BANK_DT, name="pb", tag="front")
+            nc.tensor.matmul_mx(
+                out=pb[:],
+                lhsT=xcodes[w_unit][:, t * P:(t + 1) * P].bitcast(FP8X4),
+                lhsT_scale=xscales[w_unit][:, t * P:(t + 1) * P],
+                rhs=xcodes[u][:].bitcast(FP8X4),
+                rhs_scale=xscales[u][:],
+                start=True,
+                stop=True,
+            )
+            pbank[(u, t)] = pb
+
+        def add_bias(u, t, eng):
+            if t == 0:
+                ycont[u] = work.tile([P, 4, L], BF16, name="ycont", tag="ycont")
+            b_col = bias[:, units[u][3] + t:units[u][3] + t + 1]
+            if eng == "V":
+                nc.vector.tensor_scalar(
+                    out=ycont[u][:, t, :], in0=pbank[(u, t)][:], scalar1=b_col, scalar2=None, op0=ALU.add
+                )
+            else:
+                nc.scalar.activation(out=ycont[u][:, t, :], in_=pbank[(u, t)][:], func=ACT.Identity, bias=b_col)
+
+        def interleave(u, eng):
+            yint[u] = work.tile([P, 4 * L], BF16, name="yint", tag="yint", align_bytes=64)
+            dst = yint[u][:].rearrange("p (c t) -> p c t", t=4)
+            src = ycont[u][:].rearrange("p t c -> p c t")
+            if eng == "V":
+                nc.vector.tensor_copy(out=dst, in_=src)
+            else:
+                nc.scalar.copy(out=dst, in_=src)
+
+        def quantize_out(u):
+            yc = keep.tile([P, L], U32, name="yc%d" % u, tag="yc%d" % u, align_bytes=64)
+            ys = keep.tile([P, L], U8, name="ys%d" % u, tag="ys%d" % u, align_bytes=64)
+            nc.vector.quantize_mx(out=yc[:].bitcast(FP8X4), scales=ys[:], in_=yint[u][:])
+            codes[u] = yc
+            scales[u] = ys
+
+        def product(a, b, j):
+            qu = 3 + 2 * a
+            ku = 1 if b == 0 else 2 + 2 * b
+            stat_u, mov_u = (qu, ku) if j < NT else (ku, qu)
+            t = j % NT
+            rb = psum_r.tile([P, L], F32, name="rb", tag="r")
+            nc.tensor.matmul_mx(
+                out=rb[:],
+                lhsT=codes[stat_u][:, t * P:(t + 1) * P].bitcast(FP8X4),
+                lhsT_scale=scales[stat_u][:, t * P:(t + 1) * P],
+                rhs=codes[mov_u][:].bitcast(FP8X4),
+                rhs_scale=scales[mov_u][:],
+                start=True,
+                stop=True,
+            )
+            rbank[(a, b, j)] = rb
+
+        def maxima(a, b, j):
+            nc.vector.tensor_reduce(
+                out=stats[:, a * NS + b, j:j + 1], in_=rbank[(a, b, j)][:], axis=AX.X, op=ALU.max
+            )
+
+        order = []
+        for n in range(NS):
+            for a in range(n):
+                order.append((a, n))
+            for b in range(n + 1):
+                order.append((n, b))
+
+        banks = []
+        for a, b in order:
+            for j in range(2 * NT):
+                banks.append((a, b, j))
+        state = {"made": 0, "ready_unit": 3}
+
+        def products_up_to(limit):
+            while state["made"] < min(limit, len(banks)):
+                a, b, j = banks[state["made"]]
+                if max(3 + 2 * a, 1 if b == 0 else 2 + 2 * b) > state["ready_unit"]:
+                    break
+                product(a, b, j)
+                state["made"] += 1
+
+        n_units = len(units)
+        with tc.manual_schedule():
+            for u in range(4):
+                for h in range(2):
+                    transposes(u, h)
+                    group(u, h, "S")
+                quantize_in(u)
+            for t in range(4):
+                project(1, t)
+                add_bias(1, t, "V" if t >= 2 else "S")
+            for t in range(4):
+                project(3, t)
+                add_bias(3, t, "S")
+            transposes(4, 0)
+            transposes(4, 1)
+            interleave(1, "V")
+            quantize_out(1)
+            group(4, 0, "S")
+            group(4, 1, "S")
+            interleave(3, "V")
+            quantize_in(4)
+            quantize_out(3)
+            transposes(5, 0)
+            transposes(5, 1)
+            project(4, 0)
+
+            products_up_to(LOOKAHEAD)
+            done = 0
+            for i in range(len(order)):
+                u = 4 + i
+                for j in range(2 * NT):
+                    if u < n_units:
+                        if j == 0:
+                            if u + 1 < n_units:
+                                group(u + 1, 0, "S")
+                                group(u + 1, 1, "S")
+                            add_bias(u, 0, "S")
+                        if j < 3:
+                            project(u, j + 1)
+                            add_bias(u, j + 1, "S")
+                        if j == 2:
+                            interleave(u, "S")
+                        if j == 3 and u + 1 < n_units:
+                            quantize_in(u + 1)
+                        if j in (4, 5) and u + 2 < n_units:
+                            transposes(u + 2, j - 4)
+                        if j == 6 and u + 1 < n_units:
+                            project(u + 1, 0)
+                    a, b, jj = banks[done]
+                    maxima(a, b, jj)
+                    done += 1
+                    if u < n_units and j == 2 * NT - 1:
+                        quantize_out(u)
+                        state["ready_unit"] = u
+                    products_up_to(done + LOOKAHEAD)
+
+        sums = const.tile([P, NS * NS], F32, name="sums", tag="sums")
+        nc.vector.tensor_reduce(out=sums[:], in_=stats[:], axis=AX.X, op=ALU.add)
+        fin = psum_f.tile([P, 8], F32, name="fin", tag="front")
+        nc.tensor.matmul(out=fin[:], lhsT=sel[:, 0, :], rhs=sums[:, 0:8], start=True, stop=False)
+        nc.tensor.matmul(out=fin[:], lhsT=sel[:, 1, :], rhs=sums[:, 8:16], start=False, stop=True)
+        res = const.tile([P, 8], F32, name="res", tag="res")
+        nc.vector.tensor_scalar(
+            out=res[:], in0=fin[:], scalar1=gain[:, 0:1], scalar2=1.0 / (2 * L), op0=ALU.mult, op1=ALU.mult
+        )
+        nc.sync.dma_start(out=out.rearrange("(x a) b -> x (a b)", x=2), in_=res[0:2, :])

@@ -18,7 +18,10 @@ L = 512
 D = 512
 NT = L // P
 BANK_DT = BF16
+S_SHARE = 384
 LOOKAHEAD = 4
+FOLDED = (6, 8, 10, 12)
+FOLD_LAG = 3
 
 FLOPS = 2 * (2 * NS * L) * D * D + 2 * (NS * L) * (NS * L) * D
 
@@ -30,6 +33,7 @@ def tile_attention_pa_kernel(tc, query_states, key_states, Wq, bq, Wk, bk, logit
         xin_pool = ctx.enter_context(tc.tile_pool(name="xin", bufs=1))
         keep = ctx.enter_context(tc.tile_pool(name="keep", bufs=1))
         work = ctx.enter_context(tc.tile_pool(name="work", bufs=3))
+        rpool = ctx.enter_context(tc.tile_pool(name="rpool", bufs=2))
         psum_f = ctx.enter_context(tc.psum_pool(name="psum_f", bufs=3))
         psum_r = ctx.enter_context(tc.psum_pool(name="psum_r", bufs=5))
 
@@ -43,8 +47,9 @@ def tile_attention_pa_kernel(tc, query_states, key_states, Wq, bq, Wk, bk, logit
             units.append((key_states[s], False, 0, 4))
             units.append((query_states[s], False, 2, 0))
 
-        ls_raw = const.tile([P, 1], BF16, name="ls_raw", tag="ls_raw")
-        nc.scalar.dma_start(out=ls_raw[:], in_=logit_scale.partition_broadcast(P))
+        warm = const.tile([P, 2], F32, name="warm", tag="warm")
+        nc.gpsimd.memset(warm[:, 0:1], 0.0)
+        nc.scalar.activation(out=warm[:, 1:2], in_=warm[:, 0:1], func=ACT.Exp)
         bq_raw = const.tile([P, 4], BF16, name="bq_raw", tag="bq_raw")
         nc.scalar.dma_start(out=bq_raw[:], in_=bq.rearrange("(p t) -> p t", t=4))
         bk_raw = const.tile([P, 4], BF16, name="bk_raw", tag="bk_raw")
@@ -57,11 +62,11 @@ def tile_attention_pa_kernel(tc, query_states, key_states, Wq, bq, Wk, bk, logit
             for h in range(2):
                 nc.sync.dma_start(out=x_sb[:, 2 * h:2 * h + 2, :], in_=rows[:, 2 * h:2 * h + 2, :])
             xin.append(x_sb)
+        ls_raw = const.tile([2, 1], BF16, name="ls_raw", tag="ls_raw")
+        nc.sync.dma_start(out=ls_raw[:], in_=logit_scale.partition_broadcast(2))
 
         ident = const.tile([P, P], F32, name="ident", tag="ident")
         make_identity(nc, ident[:])
-        gain = const.tile([P, 1], F32, name="gain", tag="gain")
-        nc.scalar.activation(out=gain[:], in_=ls_raw[:], func=ACT.Exp)
         bias = const.tile([P, 8], F32, name="bias", tag="bias")
         nc.vector.tensor_copy(out=bias[:, 0:4], in_=bq_raw[:])
         nc.vector.tensor_copy(out=bias[:, 4:8], in_=bk_raw[:])
@@ -137,14 +142,17 @@ def tile_attention_pa_kernel(tc, query_states, key_states, Wq, bq, Wk, bk, logit
             else:
                 nc.scalar.activation(out=ycont[u][:, t, :], in_=pbank[(u, t)][:], func=ACT.Identity, bias=b_col)
 
-        def interleave(u, eng):
-            yint[u] = work.tile([P, 4 * L], BF16, name="yint", tag="yint", align_bytes=64)
-            dst = yint[u][:].rearrange("p (c t) -> p c t", t=4)
-            src = ycont[u][:].rearrange("p t c -> p c t")
+        def interleave(u, eng, c0, c1):
+            if c0 == 0:
+                yint[u] = work.tile([P, 4 * L], BF16, name="yint", tag="yint", align_bytes=64)
+            dst = yint[u][:, 4 * c0:4 * c1].rearrange("p (c i t) -> p c t i", i=4, t=4)
+            src = ycont[u][:, :, c0:c1].rearrange("p t (c i) -> p c t i", i=4)
             if eng == "V":
                 nc.vector.tensor_copy(out=dst, in_=src)
-            else:
+            elif eng == "S":
                 nc.scalar.copy(out=dst, in_=src)
+            else:
+                nc.gpsimd.tensor_scalar(out=dst, in0=src, scalar1=1.0, scalar2=0.0, op0=ALU.mult, op1=ALU.add)
 
         def quantize_out(u):
             yc = keep.tile([P, L], U32, name="yc%d" % u, tag="yc%d" % u, align_bytes=64)
@@ -175,6 +183,54 @@ def tile_attention_pa_kernel(tc, query_states, key_states, Wq, bq, Wk, bk, logit
                 out=stats[:, a * NS + b, j:j + 1], in_=rbank[(a, b, j)][:], axis=AX.X, op=ALU.max
             )
 
+        kept = {}
+        folded = {}
+
+        def maxima_keep(a, b, j):
+            if j == 0:
+                kept[(a, b)] = rpool.tile([P, NT, L], F32, name="kept", tag="kept")
+            nc.vector.tensor_scalar(
+                out=kept[(a, b)][:, j, :], in0=rbank[(a, b, j)][:], scalar1=0.0, scalar2=None,
+                op0=ALU.add, op1=ALU.max, accum_out=stats[:, a * NS + b, j:j + 1],
+            )
+
+        def larger(x, y, label):
+            diff = rpool.tile([P, L], F32, name="diff_" + label, tag="diff_" + label)
+            nc.gpsimd.tensor_tensor(out=diff[:], in0=x, in1=y, op=ALU.subtract)
+            excess = rpool.tile([P, L], F32, name="excess_" + label, tag="excess_" + label)
+            nc.scalar.activation(out=excess[:], in_=diff[:], func=ACT.Relu)
+            return excess
+
+        def add_back(y, excess, label):
+            top = rpool.tile([P, L], F32, name="top_" + label, tag="top_" + label)
+            nc.gpsimd.tensor_tensor(out=top[:], in0=y, in1=excess[:], op=ALU.add)
+            return top
+
+        def fold(a, b):
+            rc = kept[(a, b)]
+            e01 = larger(rc[:, 0, :], rc[:, 1, :], "01")
+            e23 = larger(rc[:, 2, :], rc[:, 3, :], "23")
+            m01 = add_back(rc[:, 1, :], e01, "01")
+            m23 = add_back(rc[:, 3, :], e23, "23")
+            e = larger(m01[:], m23[:], "all")
+            folded[(a, b)] = add_back(m23[:], e, "all")
+
+        turned = {}
+
+        def turn_folded(a, b):
+            tb = psum_f.tile([P, L], F32, name="tb", tag="front")
+            for j in range(NT):
+                nc.tensor.transpose(tb[:, j * P:(j + 1) * P], folded[(a, b)][:, j * P:(j + 1) * P], ident[:])
+            turned[(a, b)] = tb
+
+        def column_maxima(a, b):
+            nc.vector.tensor_reduce(
+                out=stats[:, a * NS + b, NT:2 * NT],
+                in_=turned[(a, b)][:].rearrange("p (j q) -> p j q", j=NT),
+                axis=AX.X,
+                op=ALU.max,
+            )
+
         order = []
         for n in range(NS):
             for a in range(n):
@@ -183,9 +239,9 @@ def tile_attention_pa_kernel(tc, query_states, key_states, Wq, bq, Wk, bk, logit
                 order.append((n, b))
 
         banks = []
-        for a, b in order:
-            for j in range(2 * NT):
-                banks.append((a, b, j))
+        for i in range(len(order)):
+            for j in range(NT if i in FOLDED else 2 * NT):
+                banks.append((order[i][0], order[i][1], j))
         state = {"made": 0, "ready_unit": 3}
 
         def products_up_to(limit):
@@ -211,11 +267,11 @@ def tile_attention_pa_kernel(tc, query_states, key_states, Wq, bq, Wk, bk, logit
                 add_bias(3, t, "S")
             transposes(4, 0)
             transposes(4, 1)
-            interleave(1, "V")
+            interleave(1, "V", 0, L)
             quantize_out(1)
             group(4, 0, "S")
             group(4, 1, "S")
-            interleave(3, "V")
+            interleave(3, "V", 0, L)
             quantize_in(4)
             quantize_out(3)
             transposes(5, 0)
@@ -226,7 +282,7 @@ def tile_attention_pa_kernel(tc, query_states, key_states, Wq, bq, Wk, bk, logit
             done = 0
             for i in range(len(order)):
                 u = 4 + i
-                for j in range(2 * NT):
+                for j in range(NT if i in FOLDED else 2 * NT):
                     if u < n_units:
                         if j == 0:
                             if u + 1 < n_units:
@@ -237,28 +293,40 @@ def tile_attention_pa_kernel(tc, query_states, key_states, Wq, bq, Wk, bk, logit
                             project(u, j + 1)
                             add_bias(u, j + 1, "S")
                         if j == 2:
-                            interleave(u, "S")
+                            interleave(u, "S", 0, S_SHARE)
+                            interleave(u, "G", S_SHARE, L)
                         if j == 3 and u + 1 < n_units:
                             quantize_in(u + 1)
                         if j in (4, 5) and u + 2 < n_units:
                             transposes(u + 2, j - 4)
                         if j == 6 and u + 1 < n_units:
                             project(u + 1, 0)
+                    if j == 6 and i - FOLD_LAG in FOLDED:
+                        turn_folded(order[i - FOLD_LAG][0], order[i - FOLD_LAG][1])
                     a, b, jj = banks[done]
-                    maxima(a, b, jj)
+                    if i in FOLDED:
+                        maxima_keep(a, b, jj)
+                    else:
+                        maxima(a, b, jj)
                     done += 1
                     if u < n_units and j == 2 * NT - 1:
                         quantize_out(u)
                         state["ready_unit"] = u
                     products_up_to(done + LOOKAHEAD)
+                if i in FOLDED:
+                    fold(order[i][0], order[i][1])
+                if i - FOLD_LAG in FOLDED:
+                    column_maxima(order[i - FOLD_LAG][0], order[i - FOLD_LAG][1])
+            gain = const.tile([2, 1], F32, name="gain", tag="gain")
+            nc.scalar.activation(out=gain[:], in_=ls_raw[:], func=ACT.Exp)
 
         sums = const.tile([P, NS * NS], F32, name="sums", tag="sums")
         nc.vector.tensor_reduce(out=sums[:], in_=stats[:], axis=AX.X, op=ALU.add)
         fin = psum_f.tile([P, 8], F32, name="fin", tag="front")
         nc.tensor.matmul(out=fin[:], lhsT=sel[:, 0, :], rhs=sums[:, 0:8], start=True, stop=False)
         nc.tensor.matmul(out=fin[:], lhsT=sel[:, 1, :], rhs=sums[:, 8:16], start=False, stop=True)
-        res = const.tile([P, 8], F32, name="res", tag="res")
+        res = const.tile([2, 8], F32, name="res", tag="res")
         nc.vector.tensor_scalar(
-            out=res[:], in0=fin[:], scalar1=gain[:, 0:1], scalar2=1.0 / (2 * L), op0=ALU.mult, op1=ALU.mult
+            out=res[:], in0=fin[0:2, :], scalar1=gain[:, 0:1], scalar2=1.0 / (2 * L), op0=ALU.mult, op1=ALU.mult
         )
-        nc.sync.dma_start(out=out.rearrange("(x a) b -> x (a b)", x=2), in_=res[0:2, :])
+        nc.sync.dma_start(out=out.rearrange("(x a) b -> x (a b)", x=2), in_=res[:])

from contextlib import ExitStack

import concourse.mybir as mybir
from concourse.masks import make_identity

F32 = mybir.dt.float32
BF16 = mybir.dt.bfloat16
U32 = mybir.dt.uint32
U8 = mybir.dt.uint8
FP8X4 = mybir.dt.float8_e4m3fn_x4
ALU = mybir.AluOpType
ACT = mybir.ActivationFunctionType
AX = mybir.AxisListType

P = 128
NS = 4
L = 512
D = 512
NT = L // P
BANK_DT = BF16
S_SHARE = 384
LOOKAHEAD = 4
FOLDED = (6, 8, 10, 12)
FOLD_LAG = 3

FLOPS = 2 * (2 * NS * L) * D * D + 2 * (NS * L) * (NS * L) * D


def tile_attention_pa_kernel(tc, query_states, key_states, Wq, bq, Wk, bk, logit_scale, out):
    nc = tc.nc
    with ExitStack() as ctx:
        const = ctx.enter_context(tc.tile_pool(name="const", bufs=1))
        xin_pool = ctx.enter_context(tc.tile_pool(name="xin", bufs=1))
        keep = ctx.enter_context(tc.tile_pool(name="keep", bufs=1))
        work = ctx.enter_context(tc.tile_pool(name="work", bufs=3))
        rpool = ctx.enter_context(tc.tile_pool(name="rpool", bufs=2))
        psum_f = ctx.enter_context(tc.psum_pool(name="psum_f", bufs=3))
        psum_r = ctx.enter_context(tc.psum_pool(name="psum_r", bufs=5))

        units = [
            (Wk, True, 0, 0),
            (key_states[0], False, 0, 4),
            (Wq, True, 2, 0),
            (query_states[0], False, 2, 0),
        ]
        for s in range(1, NS):
            units.append((key_states[s], False, 0, 4))
            units.append((query_states[s], False, 2, 0))

        warm = const.tile([P, 2], F32, name="warm", tag="warm")
        nc.gpsimd.memset(warm[:, 0:1], 0.0)
        nc.scalar.activation(out=warm[:, 1:2], in_=warm[:, 0:1], func=ACT.Exp)
        bq_raw = const.tile([P, 4], BF16, name="bq_raw", tag="bq_raw")
        nc.scalar.dma_start(out=bq_raw[:], in_=bq.rearrange("(p t) -> p t", t=4))
        bk_raw = const.tile([P, 4], BF16, name="bk_raw", tag="bk_raw")
        nc.scalar.dma_start(out=bk_raw[:], in_=bk.rearrange("(p t) -> p t", t=4))

        xin = []
        for u in range(len(units)):
            x_sb = xin_pool.tile([P, NT, D], BF16, name="xin%d" % u, tag="xin%d" % u)
            rows = units[u][0].rearrange("(p n) k -> p n k", n=NT)
            for h in range(2):
                nc.sync.dma_start(out=x_sb[:, 2 * h:2 * h + 2, :], in_=rows[:, 2 * h:2 * h + 2, :])
            xin.append(x_sb)
        ls_raw = const.tile([2, 1], BF16, name="ls_raw", tag="ls_raw")
        nc.sync.dma_start(out=ls_raw[:], in_=logit_scale.partition_broadcast(2))

        ident = const.tile([P, P], F32, name="ident", tag="ident")
        make_identity(nc, ident[:])
        bias = const.tile([P, 8], F32, name="bias", tag="bias")
        nc.vector.tensor_copy(out=bias[:, 0:4], in_=bq_raw[:])
        nc.vector.tensor_copy(out=bias[:, 4:8], in_=bk_raw[:])
        sel = const.tile([P, 2, P], F32, name="sel", tag="sel")
        nc.vector.memset(sel[:], 0.0)
        nc.vector.memset(sel[:, 0, 0:1], 1.0)
        nc.vector.memset(sel[:, 1, 1:2], 1.0)
        stats = const.tile([P, NS * NS, 8], F32, name="stats", tag="stats")

        grouped = {}
        xbank = {}
        codes = {}
        scales = {}
        xcodes = {}
        xscales = {}
        pbank = {}
        ycont = {}
        yint = {}
        rbank = {}

        def transposes(u, h):
            words = xin[u][:].bitcast(F32)
            xt = psum_f.tile([P, 512], F32, name="xt", tag="front")
            for n in range(2):
                for w in range(2):
                    c0 = (2 * n + w) * P
                    nc.tensor.transpose(xt[:, c0:c0 + P], words[:, 2 * h + n, w:D // 2:2], ident[:])
            xbank[(u, h)] = xt

        def group(u, h, eng):
            if h == 0:
                grouped[u] = work.tile([P, 4 * L], BF16, name="grouped", tag="grouped", align_bytes=64)
            dst = grouped[u][:].bitcast(F32)[:, 512 * h:512 * (h + 1)].rearrange("p (n r w) -> p n r w", n=2, w=2)
            src = xbank[(u, h)][:].rearrange("p (n w r) -> p n r w", n=2, w=2)
            if eng == "V":
                nc.vector.tensor_copy(out=dst, in_=src)
            else:
                nc.scalar.copy(out=dst, in_=src)

        def quantize_in(u):
            if units[u][1]:
                xc = keep.tile([P, L], U32, name="wc%d" % u, tag="wc%d" % u, align_bytes=64)
                xs = keep.tile([P, L], U8, name="ws%d" % u, tag="ws%d" % u, align_bytes=64)
            else:
                xc = work.tile([P, L], U32, name="xc", tag="xc", align_bytes=64)
                xs = work.tile([P, L], U8, name="xs", tag="xs", align_bytes=64)
            nc.vector.quantize_mx(out=xc[:].bitcast(FP8X4), scales=xs[:], in_=grouped[u][:])
            xcodes[u] = xc
            xscales[u] = xs

        def project(u, t):
            w_unit = units[u][2]
            pb = psum_f.tile([P, L], BANK_DT, name="pb", tag="front")
            nc.tensor.matmul_mx(
                out=pb[:],
                lhsT=xcodes[w_unit][:, t * P:(t + 1) * P].bitcast(FP8X4),
                lhsT_scale=xscales[w_unit][:, t * P:(t + 1) * P],
                rhs=xcodes[u][:].bitcast(FP8X4),
                rhs_scale=xscales[u][:],
                start=True,
                stop=True,
            )
            pbank[(u, t)] = pb

        def add_bias(u, t, eng):
            if t == 0:
                ycont[u] = work.tile([P, 4, L], BF16, name="ycont", tag="ycont")
            b_col = bias[:, units[u][3] + t:units[u][3] + t + 1]
            if eng == "V":
                nc.vector.tensor_scalar(
                    out=ycont[u][:, t, :], in0=pbank[(u, t)][:], scalar1=b_col, scalar2=None, op0=ALU.add
                )
            else:
                nc.scalar.activation(out=ycont[u][:, t, :], in_=pbank[(u, t)][:], func=ACT.Identity, bias=b_col)

        def interleave(u, eng, c0, c1):
            if c0 == 0:
                yint[u] = work.tile([P, 4 * L], BF16, name="yint", tag="yint", align_bytes=64)
            dst = yint[u][:, 4 * c0:4 * c1].rearrange("p (c i t) -> p c t i", i=4, t=4)
            src = ycont[u][:, :, c0:c1].rearrange("p t (c i) -> p c t i", i=4)
            if eng == "V":
                nc.vector.tensor_copy(out=dst, in_=src)
            elif eng == "S":
                nc.scalar.copy(out=dst, in_=src)
            else:
                nc.gpsimd.tensor_scalar(out=dst, in0=src, scalar1=1.0, scalar2=0.0, op0=ALU.mult, op1=ALU.add)

        def quantize_out(u):
            yc = keep.tile([P, L], U32, name="yc%d" % u, tag="yc%d" % u, align_bytes=64)
            ys = keep.tile([P, L], U8, name="ys%d" % u, tag="ys%d" % u, align_bytes=64)
            nc.vector.quantize_mx(out=yc[:].bitcast(FP8X4), scales=ys[:], in_=yint[u][:])
            codes[u] = yc
            scales[u] = ys

        def product(a, b, j):
            qu = 3 + 2 * a
            ku = 1 if b == 0 else 2 + 2 * b
            stat_u, mov_u = (qu, ku) if j < NT else (ku, qu)
            t = j % NT
            rb = psum_r.tile([P, L], F32, name="rb", tag="r")
            nc.tensor.matmul_mx(
                out=rb[:],
                lhsT=codes[stat_u][:, t * P:(t + 1) * P].bitcast(FP8X4),
                lhsT_scale=scales[stat_u][:, t * P:(t + 1) * P],
                rhs=codes[mov_u][:].bitcast(FP8X4),
                rhs_scale=scales[mov_u][:],
                start=True,
                stop=True,
            )
            rbank[(a, b, j)] = rb

        def maxima(a, b, j):
            nc.vector.tensor_reduce(
                out=stats[:, a * NS + b, j:j + 1], in_=rbank[(a, b, j)][:], axis=AX.X, op=ALU.max
            )

        kept = {}
        folded = {}

        def maxima_keep(a, b, j):
            if j == 0:
                kept[(a, b)] = rpool.tile([P, NT, L], F32, name="kept", tag="kept")
            nc.vector.tensor_scalar(
                out=kept[(a, b)][:, j, :], in0=rbank[(a, b, j)][:], scalar1=0.0, scalar2=None,
                op0=ALU.add, op1=ALU.max, accum_out=stats[:, a * NS + b, j:j + 1],
            )

        def larger(x, y, label):
            diff = rpool.tile([P, L], F32, name="diff_" + label, tag="diff_" + label)
            nc.gpsimd.tensor_tensor(out=diff[:], in0=x, in1=y, op=ALU.subtract)
            excess = rpool.tile([P, L], F32, name="excess_" + label, tag="excess_" + label)
            nc.scalar.activation(out=excess[:], in_=diff[:], func=ACT.Relu)
            return excess

        def add_back(y, excess, label):
            top = rpool.tile([P, L], F32, name="top_" + label, tag="top_" + label)
            nc.gpsimd.tensor_tensor(out=top[:], in0=y, in1=excess[:], op=ALU.add)
            return top

        def fold(a, b):
            rc = kept[(a, b)]
            e01 = larger(rc[:, 0, :], rc[:, 1, :], "01")
            e23 = larger(rc[:, 2, :], rc[:, 3, :], "23")
            m01 = add_back(rc[:, 1, :], e01, "01")
            m23 = add_back(rc[:, 3, :], e23, "23")
            e = larger(m01[:], m23[:], "all")
            folded[(a, b)] = add_back(m23[:], e, "all")

        turned = {}

        def turn_folded(a, b):
            tb = psum_f.tile([P, L], F32, name="tb", tag="front")
            for j in range(NT):
                nc.tensor.transpose(tb[:, j * P:(j + 1) * P], folded[(a, b)][:, j * P:(j + 1) * P], ident[:])
            turned[(a, b)] = tb

        def column_maxima(a, b):
            nc.vector.tensor_reduce(
                out=stats[:, a * NS + b, NT:2 * NT],
                in_=turned[(a, b)][:].rearrange("p (j q) -> p j q", j=NT),
                axis=AX.X,
                op=ALU.max,
            )

        order = []
        for n in range(NS):
            for a in range(n):
                order.append((a, n))
            for b in range(n + 1):
                order.append((n, b))

        banks = []
        for i in range(len(order)):
            for j in range(NT if i in FOLDED else 2 * NT):
                banks.append((order[i][0], order[i][1], j))
        state = {"made": 0, "ready_unit": 3}

        def products_up_to(limit):
            while state["made"] < min(limit, len(banks)):
                a, b, j = banks[state["made"]]
                if max(3 + 2 * a, 1 if b == 0 else 2 + 2 * b) > state["ready_unit"]:
                    break
                product(a, b, j)
                state["made"] += 1

        n_units = len(units)
        with tc.manual_schedule():
            for u in range(4):
                for h in range(2):
                    transposes(u, h)
                    group(u, h, "S")
                quantize_in(u)
            for t in range(4):
                project(1, t)
                add_bias(1, t, "V" if t >= 2 else "S")
            for t in range(4):
                project(3, t)
                add_bias(3, t, "S")
            transposes(4, 0)
            transposes(4, 1)
            interleave(1, "V", 0, L)
            quantize_out(1)
            group(4, 0, "S")
            group(4, 1, "S")
            interleave(3, "V", 0, L)
            quantize_in(4)
            quantize_out(3)
            transposes(5, 0)
            transposes(5, 1)
            project(4, 0)

            products_up_to(LOOKAHEAD)
            done = 0
            for i in range(len(order)):
                u = 4 + i
                for j in range(NT if i in FOLDED else 2 * NT):
                    if u < n_units:
                        if j == 0:
                            if u + 1 < n_units:
                                group(u + 1, 0, "S")
                                group(u + 1, 1, "S")
                            add_bias(u, 0, "S")
                        if j < 3:
                            project(u, j + 1)
                            add_bias(u, j + 1, "S")
                        if j == 2:
                            interleave(u, "S", 0, S_SHARE)
                            interleave(u, "G", S_SHARE, L)
                        if j == 3 and u + 1 < n_units:
                            quantize_in(u + 1)
                        if j in (4, 5) and u + 2 < n_units:
                            transposes(u + 2, j - 4)
                        if j == 6 and u + 1 < n_units:
                            project(u + 1, 0)
                    if j == 6 and i - FOLD_LAG in FOLDED:
                        turn_folded(order[i - FOLD_LAG][0], order[i - FOLD_LAG][1])
                    a, b, jj = banks[done]
                    if i in FOLDED:
                        maxima_keep(a, b, jj)
                    else:
                        maxima(a, b, jj)
                    done += 1
                    if u < n_units and j == 2 * NT - 1:
                        quantize_out(u)
                        state["ready_unit"] = u
                    products_up_to(done + LOOKAHEAD)
                if i in FOLDED:
                    fold(order[i][0], order[i][1])
                if i - FOLD_LAG in FOLDED:
                    column_maxima(order[i - FOLD_LAG][0], order[i - FOLD_LAG][1])
            gain = const.tile([2, 1], F32, name="gain", tag="gain")
            nc.scalar.activation(out=gain[:], in_=ls_raw[:], func=ACT.Exp)

        sums = const.tile([P, NS * NS], F32, name="sums", tag="sums")
        nc.vector.tensor_reduce(out=sums[:], in_=stats[:], axis=AX.X, op=ALU.add)
        fin = psum_f.tile([P, 8], F32, name="fin", tag="front")
        nc.tensor.matmul(out=fin[:], lhsT=sel[:, 0, :], rhs=sums[:, 0:8], start=True, stop=False)
        nc.tensor.matmul(out=fin[:], lhsT=sel[:, 1, :], rhs=sums[:, 8:16], start=False, stop=True)
        res = const.tile([2, 8], F32, name="res", tag="res")
        nc.vector.tensor_scalar(
            out=res[:], in0=fin[0:2, :], scalar1=gain[:, 0:1], scalar2=1.0 / (2 * L), op0=ALU.mult, op1=ALU.mult
        )
        nc.sync.dma_start(out=out.rearrange("(x a) b -> x (a b)", x=2), in_=res[:])
